import numpy as np
import ml_dtypes


BF16 = ml_dtypes.bfloat16


def bf(x):
    return np.asarray(x, np.float32).astype(BF16)


def f64(x):
    return np.asarray(x).astype(np.float64)


E2M1 = np.array([0.0, 0.5, 1.0, 1.5, 2.0, 3.0, 4.0, 6.0, -0.0, -0.5, -1.0, -1.5, -2.0, -3.0, -4.0, -6.0])


def pack_weight(w, fmt):
    k, n = w.shape
    w = f64(bf(w)).reshape(k // 32, 32, n)
    amax = np.abs(w).max(1)
    if fmt == "e4m3":
        byte = np.frexp(amax)[1] - 1 + 127 - 7
    else:
        mant, ex = np.frexp(amax / 6.0)
        byte = np.where(mant > 0.5, ex, ex - 1) + 127
    byte = np.clip(np.where(amax > 0, byte, 1), 1, 254)
    scaled = (w * np.exp2(127.0 - byte)[:, None, :]).reshape(k, n).astype(np.float32)
    by_word = np.ascontiguousarray(scaled.reshape(k // 512, 128, 4, n).transpose(0, 1, 3, 2))
    if fmt == "e4m3":
        words = by_word.astype(ml_dtypes.float8_e4m3fn).view(np.uint8)
    else:
        c = by_word.astype(ml_dtypes.float4_e2m1fn).view(np.uint8) & 0xF
        words = c[..., 0::2] | (c[..., 1::2] << 4)
    return np.ascontiguousarray(words), np.ascontiguousarray(byte.astype(np.uint8).reshape(k // 512, 16, n))


def unpack_weight(words, scales, fmt):
    g, p, n, _ = words.shape
    if fmt == "e4m3":
        vals = np.ascontiguousarray(words).view(ml_dtypes.float8_e4m3fn).astype(np.float64)
    else:
        nib = np.empty((g, p, n, 4), np.uint8)
        nib[..., 0::2] = words & 0xF
        nib[..., 1::2] = words >> 4
        vals = E2M1[nib]
    vals = vals * np.repeat(np.exp2(scales.astype(np.float64) - 127.0), 8, axis=1)[..., None]
    return vals.transpose(0, 1, 3, 2).reshape(g * 512, n)

def pack4(w):
    words, scales = pack_weight(w, "e2m1")
    return words.reshape(words.shape[0], 128, -1), scales


def unpack4(words, scales):
    return unpack_weight(words.reshape(words.shape[0], 128, -1, 2), scales, "e2m1")


def kspread(k):
    return np.exp2(np.repeat(np.random.randint(-6, 7, k // 32), 32).astype(np.float64))


B, N, DIM, H, DH, PD = 2, 1024, 8192, 16, 64, 2
E = H * DH
ROT = DH // PD
INV_MIN_FREQ = 2.0 ** 6


def rot_freqs(t):
    inv_freq = 1.0 / (10000.0 ** (np.arange(0, ROT, 2) / ROT))
    f = (t * INV_MIN_FREQ)[..., None] * inv_freq
    return np.concatenate([f, f], axis=-1)


def rotate_half(x):
    x1, x2 = np.split(x, 2, axis=-1)
    return np.concatenate([-x2, x1], axis=-1)


def apply_rotary(t, freqs):
    return t * np.cos(freqs) + rotate_half(t) * np.sin(freqs)


def rope_2d(t, pos):
    fx = rot_freqs(pos[..., 0])[:, None]
    fy = rot_freqs(pos[..., 1])[:, None]
    return np.concatenate([apply_rotary(t[..., :ROT], fx), apply_rotary(t[..., ROT:], fy)], axis=-1)


def setup_inputs():
    s = kspread(DIM)
    u_x = np.random.standard_normal((B, N, DIM)) * s
    u_x_words, u_x_scales = pack4(np.ascontiguousarray(u_x.reshape(B * N, DIM).T))
    pos_x = bf(np.random.uniform(size=(1, N, PD)))
    Wq = np.random.standard_normal((E, DIM)) / np.sqrt(DIM) / s
    words, scales = pack4(np.ascontiguousarray(Wq.T))
    return {"u_x_words": u_x_words,
            "u_x_scales": u_x_scales,
            "pos_x": pos_x,
            "Wq_words": words,
            "Wq_scales": scales}


def reference(u_x_words, u_x_scales, pos_x, Wq_words, Wq_scales):
    y = unpack4(u_x_words, u_x_scales).T.reshape(B, N, DIM) @ unpack4(Wq_words, Wq_scales)
    q = y.reshape(B, N, H, DH).transpose(0, 2, 1, 3)
    return rope_2d(q, f64(pos_x))

@@ -1,0 +1,197 @@
+from contextlib import ExitStack
+
+import concourse.mybir as mybir
+
+F32 = mybir.dt.float32
+BF16 = mybir.dt.bfloat16
+I32 = mybir.dt.int32
+U8 = mybir.dt.uint8
+FP4X4 = mybir.dt.float4_e2m1fn_x4
+ALU = mybir.AluOpType
+ACT = mybir.ActivationFunctionType
+
+P = 128
+PASSES = 16
+TOKEN_TILES = 16
+GROUP = 4
+GROUP_COLS = GROUP * P
+CHANNELS = 1024
+BANK = 512
+HEAD = 64
+POS_TILES = 8
+
+FLOPS = 2 * 2048 * 1024 * 8192
+
+RUNS = ((0, 1), (1, 3), (3, 7), (7, 11), (11, 16))
+MERGED_FROM_RUN = 3
+CHUNK = 4
+LAST_WIDTHS = (256, 128, 128)
+WARM = 8
+
+PI = 3.141592653589793
+TURNS_PER_COORD = tuple(64.0 * 10000.0 ** (-j / 16.0) / (2.0 * PI) for j in range(16))
+
+
+def tile_asymetrickernel_pb_kernel(tc, u_x_words, u_x_scales, pos_x, Wq_words, Wq_scales, out):
+    nc = tc.nc
+
+    with ExitStack() as ctx:
+        keep = ctx.enter_context(tc.tile_pool(name="keep", bufs=1))
+        work = ctx.enter_context(tc.tile_pool(name="work", bufs=4))
+        psum = ctx.enter_context(tc.psum_pool(name="psum", bufs=8))
+        ctx.enter_context(tc.manual_schedule())
+
+        u_codes = {}
+        u_scale = {}
+        w_codes = {}
+        w_scale = {}
+
+        def load_scale_rows(planes, scales, g0, g1, c0, c1):
+            nc.vector.memset(planes[:].bitcast(I32), 0)
+            for r in range(4):
+                nc.sync.dma_start(
+                    out=planes[r:P:32, :, :].bitcast(I32),
+                    in_=scales[g0:g1, r:16:4, c0:c1].rearrange("g q n -> q g n").bitcast(I32),
+                )
+
+        def load_u_codes(group, g0, g1):
+            codes = keep.tile([P, g1 - g0, 2 * GROUP_COLS], U8, name="uc%d_%d" % (group, g0), align_bytes=64)
+            b0 = 2 * GROUP_COLS * group
+            nc.sync.dma_start(
+                out=codes[:].bitcast(I32),
+                in_=u_x_words[g0:g1, :, b0 : b0 + 2 * GROUP_COLS].rearrange("g p n -> p g n").bitcast(I32),
+            )
+            for g in range(g0, g1):
+                for i in range(GROUP):
+                    u_codes[(GROUP * group + i, g)] = codes[:, g - g0, 2 * P * i : 2 * P * (i + 1)]
+
+        def load_u_scales(group, g0, g1):
+            planes = keep.tile([P, g1 - g0, GROUP_COLS], U8, name="us%d_%d" % (group, g0), align_bytes=64)
+            load_scale_rows(planes, u_x_scales, g0, g1, GROUP_COLS * group, GROUP_COLS * (group + 1))
+            for g in range(g0, g1):
+                for i in range(GROUP):
+                    u_scale[(GROUP * group + i, g)] = planes[:, g - g0, P * i : P * (i + 1)]
+
+        def load_w_codes(g):
+            codes = keep.tile([P, 2 * CHANNELS], U8, name="wc%d" % g, align_bytes=64)
+            nc.sync.dma_start(out=codes[:].bitcast(I32), in_=Wq_words[g].bitcast(I32))
+            w_codes[g] = codes
+
+        def load_w_scales(g0, g1):
+            planes = keep.tile([P, g1 - g0, CHANNELS], U8, name="ws%d" % g0, align_bytes=64)
+            load_scale_rows(planes, Wq_scales, g0, g1, 0, CHANNELS)
+            for g in range(g0, g1):
+                w_scale[g] = planes[:, g - g0, :]
+
+        warm_in = keep.tile([P, BANK], BF16, name="warm_in")
+        nc.gpsimd.memset(warm_in[:], 0.0)
+        warm_out = psum.tile([P, BANK], F32, name="warm_out", tag="acc")
+        for i in range(WARM):
+            nc.tensor.matmul(out=warm_out[:], lhsT=warm_in[:, 0:P], rhs=warm_in[:], start=True, stop=True)
+
+        pos = keep.tile([P, POS_TILES, 2], BF16, name="pos")
+        for run, (g0, g1) in enumerate(RUNS):
+            if run == 0:
+                load_u_codes(0, 0, 1)
+                load_w_codes(0)
+            load_u_scales(0, g0, g1)
+            load_w_scales(g0, g1)
+            if run >= MERGED_FROM_RUN:
+                load_u_codes(0, g0, g1)
+            for g in range(g0, g1):
+                if run > 0:
+                    if run < MERGED_FROM_RUN:
+                        load_u_codes(0, g, g + 1)
+                    load_w_codes(g)
+            if run == 2:
+                nc.sync.dma_start(out=pos[:], in_=pos_x[0].rearrange("(t p) a -> p t a", p=P))
+        for group in range(1, TOKEN_TILES // GROUP):
+            load_u_scales(group, 0, PASSES)
+            for g0 in range(0, PASSES, CHUNK):
+                load_u_codes(group, g0, g0 + CHUNK)
+
+        turns = keep.tile([P, 2, 2 * POS_TILES, 16], F32, name="turns")
+        pos_flat = pos[:].rearrange("p t a -> p (t a)")
+        for j in range(16):
+            nc.vector.tensor_scalar(
+                out=turns[:, 0, :, j], in0=pos_flat, scalar1=TURNS_PER_COORD[j], scalar2=0.25, op0=ALU.mult, op1=ALU.add
+            )
+        nc.vector.tensor_scalar_add(out=turns[:, 1], in0=turns[:, 0], scalar1=0.25)
+        turns_flat = turns[:].rearrange("p k g j -> p (k g j)")
+        whole_i = keep.tile([P, 512], I32, name="whole_i")
+        nc.vector.tensor_copy(out=whole_i[:], in_=turns_flat)
+        whole_f = keep.tile([P, 512], F32, name="whole_f")
+        nc.vector.tensor_copy(out=whole_f[:], in_=whole_i[:])
+        frac = keep.tile([P, 512], F32, name="frac")
+        nc.vector.tensor_tensor(out=frac[:], in0=turns_flat, in1=whole_f[:], op=ALU.subtract)
+        mag = keep.tile([P, 512], F32, name="mag")
+        nc.vector.scalar_tensor_tensor(out=mag[:], in0=frac[:], scalar=-1.0, in1=frac[:], op0=ALU.mult, op1=ALU.max)
+        dist = keep.tile([P, 512], F32, name="dist")
+        nc.vector.tensor_scalar_add(out=dist[:], in0=mag[:], scalar1=-0.5)
+        fold = keep.tile([P, 512], F32, name="fold")
+        nc.vector.scalar_tensor_tensor(out=fold[:], in0=dist[:], scalar=-1.0, in1=dist[:], op0=ALU.mult, op1=ALU.max)
+        trig = keep.tile([P, 2, 2 * POS_TILES, 16], F32, name="trig")
+        nc.scalar.activation(
+            out=trig[:].rearrange("p k g j -> p (k g j)"), in_=fold[:], func=ACT.Sin, bias=PI / 2.0, scale=-2.0 * PI
+        )
+        cos_t = keep.tile([P, POS_TILES, 1, HEAD], F32, name="cos_t")
+        sin_t = keep.tile([P, POS_TILES, 1, HEAD], F32, name="sin_t")
+        cos_v = cos_t[:].rearrange("p t o (a x j) -> p (t o a) x j", x=2, j=16)
+        sin_v = sin_t[:].rearrange("p t o (a x j) -> p (t o a) x j", x=2, j=16)
+        nc.vector.tensor_copy(out=cos_v[:, :, 0, :], in_=trig[:, 1])
+        nc.vector.tensor_copy(out=cos_v[:, :, 1, :], in_=trig[:, 1])
+        nc.vector.tensor_copy(out=sin_v[:, :, 0, :], in_=trig[:, 0])
+        nc.vector.tensor_scalar_mul(out=sin_v[:, :, 1, :], in0=trig[:, 0], scalar1=-1.0)
+
+        def mx_pass(acc, m, g, c0, width):
+            nc.tensor.matmul_mx(
+                out=acc[:],
+                lhsT=u_codes[(m, g)].bitcast(FP4X4),
+                lhsT_scale=u_scale[(m, g)],
+                rhs=w_codes[g][:, 2 * c0 : 2 * (c0 + width)].bitcast(FP4X4),
+                rhs_scale=w_scale[g][:, c0 : c0 + width],
+                start=(g == 0),
+                stop=(g == PASSES - 1),
+            )
+
+        def rotate_and_store(acc, m, c0, width):
+            heads = width // HEAD
+            t = m % POS_TILES
+            b = m // POS_TILES
+            y = acc[:].rearrange("p (h c) -> p h c", c=HEAD)
+            by_cos = work.tile([P, heads, HEAD], F32, name="by_cos", tag="by_cos")
+            nc.vector.tensor_tensor(out=by_cos[:], in0=y, in1=cos_t[:, t].to_broadcast([P, heads, HEAD]), op=ALU.mult)
+            by_sin = work.tile([P, heads, HEAD], F32, name="by_sin", tag="by_sin")
+            nc.vector.tensor_tensor(out=by_sin[:], in0=y, in1=sin_t[:, t].to_broadcast([P, heads, HEAD]), op=ALU.mult)
+            rot = work.tile([P, heads, HEAD], F32, name="rot", tag="rot")
+            c_v = by_cos[:].rearrange("p h (a x j) -> p (h a) x j", x=2, j=16)
+            s_v = by_sin[:].rearrange("p h (a x j) -> p (h a) x j", x=2, j=16)
+            r_v = rot[:].rearrange("p h (a x j) -> p (h a) x j", x=2, j=16)
+            for x in range(2):
+                nc.vector.tensor_tensor(out=r_v[:, :, x, :], in0=c_v[:, :, x, :], in1=s_v[:, :, 1 - x, :], op=ALU.add)
+            h0 = c0 // HEAD
+            nc.scalar.dma_start(
+                out=out[b, h0 : h0 + heads, P * t : P * (t + 1), :].rearrange("h i c -> i h c"), in_=rot[:]
+            )
+
+        first = [(m, c0) for m in range(GROUP) for c0 in range(0, CHANNELS, BANK)]
+        accs = {}
+        for key in first:
+            accs[key] = psum.tile([P, BANK], F32, name="acc", tag="acc")
+        for g in range(PASSES):
+            for m, c0 in first:
+                mx_pass(accs[(m, c0)], m, g, c0, BANK)
+                if g == PASSES - 1:
+                    rotate_and_store(accs[(m, c0)], m, c0, BANK)
+
+        rest = [(m, c0, BANK) for m in range(GROUP, TOKEN_TILES) for c0 in range(0, CHANNELS, BANK)]
+        rest = rest[: len(rest) - 1]
+        c0 = BANK
+        for width in LAST_WIDTHS:
+            rest.append((TOKEN_TILES - 1, c0, width))
+            c0 += width
+        for m, c0, width in rest:
+            acc = psum.tile([P, width], F32, name="acc", tag="acc")
+            for g in range(PASSES):
+                mx_pass(acc, m, g, c0, width)
+            rotate_and_store(acc, m, c0, width)

@@ -17,16 +17,17 @@ GROUP = 4
 GROUP_COLS = GROUP * P
 CHANNELS = 1024
 BANK = 512
+BLOCKS = CHANNELS // BANK
 HEAD = 64
 POS_TILES = 8
 
 FLOPS = 2 * 2048 * 1024 * 8192
 
-RUNS = ((0, 1), (1, 3), (3, 7), (7, 11), (11, 16))
-MERGED_FROM_RUN = 3
+RUN_LENGTHS = (2, 2, 2, 3, 3, 4)
+POS_AFTER_RUN = 3
 CHUNK = 4
 LAST_WIDTHS = (256, 128, 128)
-WARM = 8
+WARM = 7
 
 PI = 3.141592653589793
 TURNS_PER_COORD = tuple(64.0 * 10000.0 ** (-j / 16.0) / (2.0 * PI) for j in range(16))
@@ -72,43 +73,50 @@ def tile_asymetrickernel_pb_kernel(tc, u_x_words, u_x_scales, pos_x, Wq_words, W
                 for i in range(GROUP):
                     u_scale[(GROUP * group + i, g)] = planes[:, g - g0, P * i : P * (i + 1)]
 
-        def load_w_codes(g):
-            codes = keep.tile([P, 2 * CHANNELS], U8, name="wc%d" % g, align_bytes=64)
-            nc.sync.dma_start(out=codes[:].bitcast(I32), in_=Wq_words[g].bitcast(I32))
-            w_codes[g] = codes
+        def load_w_codes(g, blk0, blk1):
+            codes = keep.tile([P, 2 * BANK * (blk1 - blk0)], U8, name="wc%d_%d" % (g, blk0), align_bytes=64)
+            nc.sync.dma_start(
+                out=codes[:].bitcast(I32), in_=Wq_words[g, :, 2 * BANK * blk0 : 2 * BANK * blk1].bitcast(I32)
+            )
+            for blk in range(blk0, blk1):
+                w_codes[(g, blk)] = codes[:, 2 * BANK * (blk - blk0) : 2 * BANK * (blk - blk0 + 1)]
 
         def load_w_scales(g0, g1):
             planes = keep.tile([P, g1 - g0, CHANNELS], U8, name="ws%d" % g0, align_bytes=64)
             load_scale_rows(planes, Wq_scales, g0, g1, 0, CHANNELS)
             for g in range(g0, g1):
-                w_scale[g] = planes[:, g - g0, :]
+                for blk in range(BLOCKS):
+                    w_scale[(g, blk)] = planes[:, g - g0, BANK * blk : BANK * (blk + 1)]
 
         warm_in = keep.tile([P, BANK], BF16, name="warm_in")
-        nc.gpsimd.memset(warm_in[:], 0.0)
+        nc.vector.memset(warm_in[:], 0.0)
         warm_out = psum.tile([P, BANK], F32, name="warm_out", tag="acc")
         for i in range(WARM):
             nc.tensor.matmul(out=warm_out[:], lhsT=warm_in[:, 0:P], rhs=warm_in[:], start=True, stop=True)
 
         pos = keep.tile([P, POS_TILES, 2], BF16, name="pos")
-        for run, (g0, g1) in enumerate(RUNS):
+        g0 = 0
+        for run, length in enumerate(RUN_LENGTHS):
+            g1 = g0 + length
             if run == 0:
                 load_u_codes(0, 0, 1)
-                load_w_codes(0)
+                load_w_codes(0, 0, 1)
             load_u_scales(0, g0, g1)
             load_w_scales(g0, g1)
-            if run >= MERGED_FROM_RUN:
+            if run == 0:
+                load_w_codes(0, 1, BLOCKS)
+                load_u_codes(0, 1, g1)
+            else:
                 load_u_codes(0, g0, g1)
-            for g in range(g0, g1):
-                if run > 0:
-                    if run < MERGED_FROM_RUN:
-                        load_u_codes(0, g, g + 1)
-                    load_w_codes(g)
-            if run == 2:
+            for g in range(max(g0, 1), g1):
+                load_w_codes(g, 0, BLOCKS)
+            if run == POS_AFTER_RUN:
                 nc.sync.dma_start(out=pos[:], in_=pos_x[0].rearrange("(t p) a -> p t a", p=P))
+            g0 = g1
         for group in range(1, TOKEN_TILES // GROUP):
             load_u_scales(group, 0, PASSES)
-            for g0 in range(0, PASSES, CHUNK):
-                load_u_codes(group, g0, g0 + CHUNK)
+            for c in range(0, PASSES, CHUNK):
+                load_u_codes(group, c, c + CHUNK)
 
         turns = keep.tile([P, 2, 2 * POS_TILES, 16], F32, name="turns")
         pos_flat = pos[:].rearrange("p t a -> p (t a)")
@@ -143,18 +151,18 @@ def tile_asymetrickernel_pb_kernel(tc, u_x_words, u_x_scales, pos_x, Wq_words, W
         nc.vector.tensor_copy(out=sin_v[:, :, 0, :], in_=trig[:, 0])
         nc.vector.tensor_scalar_mul(out=sin_v[:, :, 1, :], in0=trig[:, 0], scalar1=-1.0)
 
-        def mx_pass(acc, m, g, c0, width):
+        def mx_pass(acc, m, g, blk, c0, width):
             nc.tensor.matmul_mx(
                 out=acc[:],
                 lhsT=u_codes[(m, g)].bitcast(FP4X4),
                 lhsT_scale=u_scale[(m, g)],
-                rhs=w_codes[g][:, 2 * c0 : 2 * (c0 + width)].bitcast(FP4X4),
-                rhs_scale=w_scale[g][:, c0 : c0 + width],
+                rhs=w_codes[(g, blk)][:, 2 * c0 : 2 * (c0 + width)].bitcast(FP4X4),
+                rhs_scale=w_scale[(g, blk)][:, c0 : c0 + width],
                 start=(g == 0),
                 stop=(g == PASSES - 1),
             )
 
-        def rotate_and_store(acc, m, c0, width):
+        def rotate_and_store(acc, m, blk, c0, width):
             heads = width // HEAD
             t = m % POS_TILES
             b = m // POS_TILES
@@ -167,31 +175,30 @@ def tile_asymetrickernel_pb_kernel(tc, u_x_words, u_x_scales, pos_x, Wq_words, W
             c_v = by_cos[:].rearrange("p h (a x j) -> p (h a) x j", x=2, j=16)
             s_v = by_sin[:].rearrange("p h (a x j) -> p (h a) x j", x=2, j=16)
             r_v = rot[:].rearrange("p h (a x j) -> p (h a) x j", x=2, j=16)
-            for x in range(2):
-                nc.vector.tensor_tensor(out=r_v[:, :, x, :], in0=c_v[:, :, x, :], in1=s_v[:, :, 1 - x, :], op=ALU.add)
-            h0 = c0 // HEAD
+            nc.vector.tensor_tensor(out=r_v, in0=c_v, in1=s_v[:, :, ::-1, :], op=ALU.add)
+            h0 = (BANK * blk + c0) // HEAD
             nc.scalar.dma_start(
                 out=out[b, h0 : h0 + heads, P * t : P * (t + 1), :].rearrange("h i c -> i h c"), in_=rot[:]
             )
 
-        first = [(m, c0) for m in range(GROUP) for c0 in range(0, CHANNELS, BANK)]
+        first = [(m, blk) for blk in range(BLOCKS) for m in range(GROUP)]
         accs = {}
         for key in first:
             accs[key] = psum.tile([P, BANK], F32, name="acc", tag="acc")
         for g in range(PASSES):
-            for m, c0 in first:
-                mx_pass(accs[(m, c0)], m, g, c0, BANK)
+            for m, blk in first:
+                mx_pass(accs[(m, blk)], m, g, blk, 0, BANK)
                 if g == PASSES - 1:
-                    rotate_and_store(accs[(m, c0)], m, c0, BANK)
+                    rotate_and_store(accs[(m, blk)], m, blk, 0, BANK)
 
-        rest = [(m, c0, BANK) for m in range(GROUP, TOKEN_TILES) for c0 in range(0, CHANNELS, BANK)]
+        rest = [(m, blk, 0, BANK) for m in range(GROUP, TOKEN_TILES) for blk in range(BLOCKS)]
         rest = rest[: len(rest) - 1]
-        c0 = BANK
+        c0 = 0
         for width in LAST_WIDTHS:
-            rest.append((TOKEN_TILES - 1, c0, width))
+            rest.append((TOKEN_TILES - 1, BLOCKS - 1, c0, width))
             c0 += width
-        for m, c0, width in rest:
+        for m, blk, c0, width in rest:
             acc = psum.tile([P, width], F32, name="acc", tag="acc")
             for g in range(PASSES):
-                mx_pass(acc, m, g, c0, width)
-            rotate_and_store(acc, m, c0, width)
+                mx_pass(acc, m, g, blk, c0, width)
+            rotate_and_store(acc, m, blk, c0, width)

@@ -27,7 +27,7 @@ RUN_LENGTHS = (2, 2, 2, 3, 3, 4)
 POS_AFTER_RUN = 3
 CHUNK = 4
 LAST_WIDTHS = (256, 128, 128)
-WARM = 7
+WARM = 4
 
 PI = 3.141592653589793
 TURNS_PER_COORD = tuple(64.0 * 10000.0 ** (-j / 16.0) / (2.0 * PI) for j in range(16))

@@ -88,22 +88,20 @@ def tile_asymetrickernel_pb_kernel(tc, u_x_words, u_x_scales, pos_x, Wq_words, W
                 for blk in range(BLOCKS):
                     w_scale[(g, blk)] = planes[:, g - g0, BANK * blk : BANK * (blk + 1)]
 
-        warm_in = keep.tile([P, BANK], BF16, name="warm_in")
-        nc.vector.memset(warm_in[:], 0.0)
-        warm_out = psum.tile([P, BANK], F32, name="warm_out", tag="acc")
-        for i in range(WARM):
-            nc.tensor.matmul(out=warm_out[:], lhsT=warm_in[:, 0:P], rhs=warm_in[:], start=True, stop=True)
-
         pos = keep.tile([P, POS_TILES, 2], BF16, name="pos")
         g0 = 0
         for run, length in enumerate(RUN_LENGTHS):
             g1 = g0 + length
-            if run == 0:
-                load_u_codes(0, 0, 1)
-                load_w_codes(0, 0, 1)
             load_u_scales(0, g0, g1)
             load_w_scales(g0, g1)
             if run == 0:
+                warm_in = keep.tile([P, BANK], BF16, name="warm_in")
+                nc.vector.memset(warm_in[:], 0.0)
+                warm_out = psum.tile([P, BANK], F32, name="warm_out", tag="acc")
+                for i in range(WARM):
+                    nc.tensor.matmul(out=warm_out[:], lhsT=warm_in[:, 0:P], rhs=warm_in[:], start=True, stop=True)
+                load_u_codes(0, 0, 1)
+                load_w_codes(0, 0, 1)
                 load_w_codes(0, 1, BLOCKS)
                 load_u_codes(0, 1, g1)
             else:

from contextlib import ExitStack

import concourse.mybir as mybir

F32 = mybir.dt.float32
BF16 = mybir.dt.bfloat16
I32 = mybir.dt.int32
U8 = mybir.dt.uint8
FP4X4 = mybir.dt.float4_e2m1fn_x4
ALU = mybir.AluOpType
ACT = mybir.ActivationFunctionType

P = 128
PASSES = 16
TOKEN_TILES = 16
GROUP = 4
GROUP_COLS = GROUP * P
CHANNELS = 1024
BANK = 512
BLOCKS = CHANNELS // BANK
HEAD = 64
POS_TILES = 8

FLOPS = 2 * 2048 * 1024 * 8192

RUN_LENGTHS = (2, 2, 2, 3, 3, 4)
POS_AFTER_RUN = 3
CHUNK = 4
LAST_WIDTHS = (256, 128, 128)
WARM = 4

PI = 3.141592653589793
TURNS_PER_COORD = tuple(64.0 * 10000.0 ** (-j / 16.0) / (2.0 * PI) for j in range(16))


def tile_asymetrickernel_pb_kernel(tc, u_x_words, u_x_scales, pos_x, Wq_words, Wq_scales, out):
    nc = tc.nc

    with ExitStack() as ctx:
        keep = ctx.enter_context(tc.tile_pool(name="keep", bufs=1))
        work = ctx.enter_context(tc.tile_pool(name="work", bufs=4))
        psum = ctx.enter_context(tc.psum_pool(name="psum", bufs=8))
        ctx.enter_context(tc.manual_schedule())

        u_codes = {}
        u_scale = {}
        w_codes = {}
        w_scale = {}

        def load_scale_rows(planes, scales, g0, g1, c0, c1):
            nc.vector.memset(planes[:].bitcast(I32), 0)
            for r in range(4):
                nc.sync.dma_start(
                    out=planes[r:P:32, :, :].bitcast(I32),
                    in_=scales[g0:g1, r:16:4, c0:c1].rearrange("g q n -> q g n").bitcast(I32),
                )

        def load_u_codes(group, g0, g1):
            codes = keep.tile([P, g1 - g0, 2 * GROUP_COLS], U8, name="uc%d_%d" % (group, g0), align_bytes=64)
            b0 = 2 * GROUP_COLS * group
            nc.sync.dma_start(
                out=codes[:].bitcast(I32),
                in_=u_x_words[g0:g1, :, b0 : b0 + 2 * GROUP_COLS].rearrange("g p n -> p g n").bitcast(I32),
            )
            for g in range(g0, g1):
                for i in range(GROUP):
                    u_codes[(GROUP * group + i, g)] = codes[:, g - g0, 2 * P * i : 2 * P * (i + 1)]

        def load_u_scales(group, g0, g1):
            planes = keep.tile([P, g1 - g0, GROUP_COLS], U8, name="us%d_%d" % (group, g0), align_bytes=64)
            load_scale_rows(planes, u_x_scales, g0, g1, GROUP_COLS * group, GROUP_COLS * (group + 1))
            for g in range(g0, g1):
                for i in range(GROUP):
                    u_scale[(GROUP * group + i, g)] = planes[:, g - g0, P * i : P * (i + 1)]

        def load_w_codes(g, blk0, blk1):
            codes = keep.tile([P, 2 * BANK * (blk1 - blk0)], U8, name="wc%d_%d" % (g, blk0), align_bytes=64)
            nc.sync.dma_start(
                out=codes[:].bitcast(I32), in_=Wq_words[g, :, 2 * BANK * blk0 : 2 * BANK * blk1].bitcast(I32)
            )
            for blk in range(blk0, blk1):
                w_codes[(g, blk)] = codes[:, 2 * BANK * (blk - blk0) : 2 * BANK * (blk - blk0 + 1)]

        def load_w_scales(g0, g1):
            planes = keep.tile([P, g1 - g0, CHANNELS], U8, name="ws%d" % g0, align_bytes=64)
            load_scale_rows(planes, Wq_scales, g0, g1, 0, CHANNELS)
            for g in range(g0, g1):
                for blk in range(BLOCKS):
                    w_scale[(g, blk)] = planes[:, g - g0, BANK * blk : BANK * (blk + 1)]

        pos = keep.tile([P, POS_TILES, 2], BF16, name="pos")
        g0 = 0
        for run, length in enumerate(RUN_LENGTHS):
            g1 = g0 + length
            load_u_scales(0, g0, g1)
            load_w_scales(g0, g1)
            if run == 0:
                warm_in = keep.tile([P, BANK], BF16, name="warm_in")
                nc.vector.memset(warm_in[:], 0.0)
                warm_out = psum.tile([P, BANK], F32, name="warm_out", tag="acc")
                for i in range(WARM):
                    nc.tensor.matmul(out=warm_out[:], lhsT=warm_in[:, 0:P], rhs=warm_in[:], start=True, stop=True)
                load_u_codes(0, 0, 1)
                load_w_codes(0, 0, 1)
                load_w_codes(0, 1, BLOCKS)
                load_u_codes(0, 1, g1)
            else:
                load_u_codes(0, g0, g1)
            for g in range(max(g0, 1), g1):
                load_w_codes(g, 0, BLOCKS)
            if run == POS_AFTER_RUN:
                nc.sync.dma_start(out=pos[:], in_=pos_x[0].rearrange("(t p) a -> p t a", p=P))
            g0 = g1
        for group in range(1, TOKEN_TILES // GROUP):
            load_u_scales(group, 0, PASSES)
            for c in range(0, PASSES, CHUNK):
                load_u_codes(group, c, c + CHUNK)

        turns = keep.tile([P, 2, 2 * POS_TILES, 16], F32, name="turns")
        pos_flat = pos[:].rearrange("p t a -> p (t a)")
        for j in range(16):
            nc.vector.tensor_scalar(
                out=turns[:, 0, :, j], in0=pos_flat, scalar1=TURNS_PER_COORD[j], scalar2=0.25, op0=ALU.mult, op1=ALU.add
            )
        nc.vector.tensor_scalar_add(out=turns[:, 1], in0=turns[:, 0], scalar1=0.25)
        turns_flat = turns[:].rearrange("p k g j -> p (k g j)")
        whole_i = keep.tile([P, 512], I32, name="whole_i")
        nc.vector.tensor_copy(out=whole_i[:], in_=turns_flat)
        whole_f = keep.tile([P, 512], F32, name="whole_f")
        nc.vector.tensor_copy(out=whole_f[:], in_=whole_i[:])
        frac = keep.tile([P, 512], F32, name="frac")
        nc.vector.tensor_tensor(out=frac[:], in0=turns_flat, in1=whole_f[:], op=ALU.subtract)
        mag = keep.tile([P, 512], F32, name="mag")
        nc.vector.scalar_tensor_tensor(out=mag[:], in0=frac[:], scalar=-1.0, in1=frac[:], op0=ALU.mult, op1=ALU.max)
        dist = keep.tile([P, 512], F32, name="dist")
        nc.vector.tensor_scalar_add(out=dist[:], in0=mag[:], scalar1=-0.5)
        fold = keep.tile([P, 512], F32, name="fold")
        nc.vector.scalar_tensor_tensor(out=fold[:], in0=dist[:], scalar=-1.0, in1=dist[:], op0=ALU.mult, op1=ALU.max)
        trig = keep.tile([P, 2, 2 * POS_TILES, 16], F32, name="trig")
        nc.scalar.activation(
            out=trig[:].rearrange("p k g j -> p (k g j)"), in_=fold[:], func=ACT.Sin, bias=PI / 2.0, scale=-2.0 * PI
        )
        cos_t = keep.tile([P, POS_TILES, 1, HEAD], F32, name="cos_t")
        sin_t = keep.tile([P, POS_TILES, 1, HEAD], F32, name="sin_t")
        cos_v = cos_t[:].rearrange("p t o (a x j) -> p (t o a) x j", x=2, j=16)
        sin_v = sin_t[:].rearrange("p t o (a x j) -> p (t o a) x j", x=2, j=16)
        nc.vector.tensor_copy(out=cos_v[:, :, 0, :], in_=trig[:, 1])
        nc.vector.tensor_copy(out=cos_v[:, :, 1, :], in_=trig[:, 1])
        nc.vector.tensor_copy(out=sin_v[:, :, 0, :], in_=trig[:, 0])
        nc.vector.tensor_scalar_mul(out=sin_v[:, :, 1, :], in0=trig[:, 0], scalar1=-1.0)

        def mx_pass(acc, m, g, blk, c0, width):
            nc.tensor.matmul_mx(
                out=acc[:],
                lhsT=u_codes[(m, g)].bitcast(FP4X4),
                lhsT_scale=u_scale[(m, g)],
                rhs=w_codes[(g, blk)][:, 2 * c0 : 2 * (c0 + width)].bitcast(FP4X4),
                rhs_scale=w_scale[(g, blk)][:, c0 : c0 + width],
                start=(g == 0),
                stop=(g == PASSES - 1),
            )

        def rotate_and_store(acc, m, blk, c0, width):
            heads = width // HEAD
            t = m % POS_TILES
            b = m // POS_TILES
            y = acc[:].rearrange("p (h c) -> p h c", c=HEAD)
            by_cos = work.tile([P, heads, HEAD], F32, name="by_cos", tag="by_cos")
            nc.vector.tensor_tensor(out=by_cos[:], in0=y, in1=cos_t[:, t].to_broadcast([P, heads, HEAD]), op=ALU.mult)
            by_sin = work.tile([P, heads, HEAD], F32, name="by_sin", tag="by_sin")
            nc.vector.tensor_tensor(out=by_sin[:], in0=y, in1=sin_t[:, t].to_broadcast([P, heads, HEAD]), op=ALU.mult)
            rot = work.tile([P, heads, HEAD], F32, name="rot", tag="rot")
            c_v = by_cos[:].rearrange("p h (a x j) -> p (h a) x j", x=2, j=16)
            s_v = by_sin[:].rearrange("p h (a x j) -> p (h a) x j", x=2, j=16)
            r_v = rot[:].rearrange("p h (a x j) -> p (h a) x j", x=2, j=16)
            nc.vector.tensor_tensor(out=r_v, in0=c_v, in1=s_v[:, :, ::-1, :], op=ALU.add)
            h0 = (BANK * blk + c0) // HEAD
            nc.scalar.dma_start(
                out=out[b, h0 : h0 + heads, P * t : P * (t + 1), :].rearrange("h i c -> i h c"), in_=rot[:]
            )

        first = [(m, blk) for blk in range(BLOCKS) for m in range(GROUP)]
        accs = {}
        for key in first:
            accs[key] = psum.tile([P, BANK], F32, name="acc", tag="acc")
        for g in range(PASSES):
            for m, blk in first:
                mx_pass(accs[(m, blk)], m, g, blk, 0, BANK)
                if g == PASSES - 1:
                    rotate_and_store(accs[(m, blk)], m, blk, 0, BANK)

        rest = [(m, blk, 0, BANK) for m in range(GROUP, TOKEN_TILES) for blk in range(BLOCKS)]
        rest = rest[: len(rest) - 1]
        c0 = 0
        for width in LAST_WIDTHS:
            rest.append((TOKEN_TILES - 1, BLOCKS - 1, c0, width))
            c0 += width
        for m, blk, c0, width in rest:
            acc = psum.tile([P, width], F32, name="acc", tag="acc")
            for g in range(PASSES):
                mx_pass(acc, m, g, blk, c0, width)
            rotate_and_store(acc, m, blk, c0, width)
